import numpy as np
import ml_dtypes


def mxq(x, axis, fmt="e4m3"):
    dtype, down = {"e4m3": (ml_dtypes.float8_e4m3fn, 7), "e5m2": (ml_dtypes.float8_e5m2, 14)}[fmt]
    v = np.moveaxis(np.asarray(x, np.float32).astype(ml_dtypes.bfloat16).astype(np.float64), axis, -1)
    blocks = v.reshape(v.shape[:-1] + (-1, 32))
    amax = np.abs(blocks).max(-1, keepdims=True)
    byte = np.maximum(np.where(amax > 0, np.frexp(amax)[1] - 1 + 127, 0) - down, 1)
    scale = np.exp2(byte - 127.0)
    codes = (blocks / scale).astype(np.float32).astype(dtype).astype(np.float64)
    return np.moveaxis((codes * scale).reshape(v.shape), -1, axis)


WIDE = False


def mx_kscale(k):
    if not WIDE:
        return np.ones(k)
    levels = np.array([10, -10, 5, -5, 0])
    a = np.random.permutation(np.resize(levels, k // 512 * 4)).reshape(k // 512, 4)
    idx = np.arange(k)
    return np.exp2(a[idx // 512, idx % 128 // 32])


BF16 = ml_dtypes.bfloat16


def bf(x):
    return np.asarray(x, np.float32).astype(BF16)


def f64(x):
    return np.asarray(x).astype(np.float64)


B, L, C, K, D_MODEL, H, D_LLM = 64, 64, 2, 100, 512, 32, 1024
D_KEYS = D_MODEL // H
G = H * D_KEYS


def setup_inputs():
    s = mx_kscale(G).reshape(H, D_KEYS)
    return {
        "attn_ctx": bf(np.random.standard_normal((B, C, L, H, D_KEYS)) * 0.5 * s),
        "Wo": bf(np.random.standard_normal((C, H, D_KEYS, D_LLM)) * 2.0 / np.sqrt(G) / s[:, :, None]),
        "bo": bf(np.random.standard_normal((C, D_LLM)) * 0.5),
        "cluster_probs": bf(np.random.uniform(size=(B, L, C))),
    }


def reference(attn_ctx, Wo, bo, cluster_probs):
    o = f64(attn_ctx).reshape(B, C, L, G)
    w = f64(Wo).reshape(C, G, D_LLM)
    proj = mxq(o, 3, "e4m3") @ mxq(w, 1, "e4m3")
    aligned = proj.transpose(0, 2, 1, 3) + f64(bo)
    return (aligned * f64(cluster_probs)[:, :, :, None]).sum(-2)

@@ -1,0 +1,177 @@
+from contextlib import ExitStack
+
+import concourse.mybir as mybir
+from concourse.masks import make_identity
+
+F32 = mybir.dt.float32
+BF16 = mybir.dt.bfloat16
+U32 = mybir.dt.uint32
+U8 = mybir.dt.uint8
+FP8X4 = mybir.dt.float8_e4m3fn_x4
+MULT = mybir.AluOpType.mult
+ADD = mybir.AluOpType.add
+COPY = mybir.ActivationFunctionType.Copy
+
+B = 64
+C = 2
+L = 64
+K = 512
+E = 1024
+P = 128
+PACK = 4
+WORDS = K // 2
+N_MOVE = 512
+HALVES = E // N_MOVE
+TILES = B * L // P
+CHUNK = 4
+FLOPS = 2 * B * C * L * K * E
+
+
+def tile_model_pa_t_kernel(tc, attn_ctx, Wo, bo, cluster_probs, out):
+    nc = tc.nc
+
+    out_rows = out.rearrange("b (j i) e -> (b j) i e", j=2)
+    prob_rows = cluster_probs.rearrange("b (j i) c -> (b j) (i c)", j=2)
+    attn_rows = attn_ctx.rearrange("b c (j i) h d -> (b c) j (i h d)", j=2)
+    wo_rows = Wo.rearrange("c h d e -> c (h d) e")
+
+    with ExitStack() as ctx:
+        const = ctx.enter_context(tc.tile_pool(name="const", bufs=1))
+        x_pool = ctx.enter_context(tc.tile_pool(name="x_pool", bufs=TILES // CHUNK))
+        work = ctx.enter_context(tc.tile_pool(name="work", bufs=2))
+        res_pool = ctx.enter_context(tc.tile_pool(name="res_pool", bufs=6))
+        xt_psum = ctx.enter_context(tc.psum_pool(name="xt_psum", bufs=2))
+        acc_psum = ctx.enter_context(tc.psum_pool(name="acc_psum", bufs=6))
+
+        prob_bf = const.tile([P, TILES * C], BF16)
+        nc.scalar.dma_start(out=prob_bf[:], in_=prob_rows)
+        bias_all = const.tile([P, C * E], BF16)
+        nc.scalar.dma_start(out=bias_all[:], in_=bo.rearrange("c e -> (c e)").partition_broadcast(P))
+
+        wo_raw = {}
+        x_chunks = {}
+
+        def load_wo(c):
+            raw = const.tile([P, PACK * E], BF16, name="wo_raw%d" % c)
+            nc.sync.dma_start(
+                out=raw[:].rearrange("p (u f) -> p u f", u=2),
+                in_=wo_rows[c].rearrange("(u p r) e -> p u (r e)", u=2, r=2),
+            )
+            wo_raw[c] = raw
+
+        def load_x(g):
+            x = x_pool.tile([P, 2 * CHUNK * K], BF16)
+            nc.sync.dma_start(
+                out=x[:].rearrange("p (j f) -> p j f", j=2),
+                in_=attn_rows[:, :, g * CHUNK * K : (g + 1) * CHUNK * K],
+            )
+            x_chunks[g] = x
+
+        load_wo(0)
+        load_wo(1)
+        for g in range(TILES // CHUNK):
+            load_x(g)
+
+        ident = const.tile([P, P], F32)
+        make_identity(nc, ident[:])
+        prob = const.tile([P, TILES * C], F32)
+        nc.vector.tensor_copy(out=prob[:], in_=prob_bf[:])
+
+        wo_codes = {}
+        wo_scales = {}
+        for c in range(C):
+            grouped_w = const.tile([P, E * PACK], BF16, name="wo_grouped%d" % c, align_bytes=64)
+            nc.vector.tensor_copy(
+                out=grouped_w[:].rearrange("p (n i t) -> p n t i", i=4, t=PACK),
+                in_=wo_raw[c][:].rearrange("p (t n i) -> p n t i", t=PACK, i=4),
+            )
+            codes_w = const.tile([P, E], U32, name="wo_codes%d" % c, align_bytes=64)
+            scales_w = const.tile([P, E], U8, name="wo_scales%d" % c, align_bytes=64)
+            nc.vector.quantize_mx(out=codes_w[:].bitcast(FP8X4), scales=scales_w[:], in_=grouped_w[:])
+            wo_codes[c] = codes_w
+            wo_scales[c] = scales_w
+
+        res_tiles = {}
+        grouped_tiles = {}
+        code_tiles = {}
+        acc_tiles = {}
+
+        def weight(i, c):
+            return prob[:, C * i + c : C * i + c + 1]
+
+        def mix_bias(i):
+            scaled = work.tile([P, C * E], F32)
+            for c in range(C):
+                nc.scalar.activation(
+                    out=scaled[:, c * E : (c + 1) * E],
+                    in_=bias_all[:, c * E : (c + 1) * E],
+                    func=COPY,
+                    scale=weight(i, c),
+                )
+            res = res_pool.tile([P, E], F32)
+            nc.gpsimd.tensor_tensor(out=res[:], in0=scaled[:, 0:E], in1=scaled[:, E : 2 * E], op=ADD)
+            res_tiles[i] = res
+
+        def transpose_tokens(i):
+            x_words = x_chunks[i // CHUNK][:].bitcast(F32)
+            xt = xt_psum.tile([P, PACK * P], F32)
+            for j in range(2):
+                for u in range(2):
+                    s = 2 * j + u
+                    first = (j * CHUNK + i % CHUNK) * WORDS + u * P
+                    nc.tensor.transpose(xt[:, s * P : (s + 1) * P], x_words[:, first : first + P], ident[:])
+            grouped = work.tile([P, C * P * PACK], BF16, align_bytes=64)
+            nc.scalar.copy(
+                out=grouped[:].bitcast(F32).rearrange("p (c b s) -> p c b s", c=C, s=PACK),
+                in_=xt[:].rearrange("p (s b c) -> p c b s", s=PACK, c=C),
+            )
+            grouped_tiles[i] = grouped
+
+        def quantise_tokens(i):
+            codes = work.tile([P, C * P], U32, align_bytes=64)
+            scales = work.tile([P, C * P], U8, align_bytes=64)
+            nc.vector.quantize_mx(out=codes[:].bitcast(FP8X4), scales=scales[:], in_=grouped_tiles[i][:])
+            code_tiles[i] = (codes, scales)
+
+        def multiply(i):
+            codes, scales = code_tiles[i]
+            for c in range(C):
+                for h in range(HALVES):
+                    acc = acc_psum.tile([P, N_MOVE], F32)
+                    nc.tensor.matmul_mx(
+                        out=acc[:],
+                        lhsT=codes[:, c * P : (c + 1) * P].bitcast(FP8X4),
+                        lhsT_scale=scales[:, c * P : (c + 1) * P],
+                        rhs=wo_codes[c][:, h * N_MOVE : (h + 1) * N_MOVE].bitcast(FP8X4),
+                        rhs_scale=wo_scales[c][:, h * N_MOVE : (h + 1) * N_MOVE],
+                        start=True,
+                        stop=True,
+                    )
+                    acc_tiles[(i, c, h)] = acc
+
+        def combine(i):
+            res = res_tiles[i]
+            for c in range(C):
+                for h in range(HALVES):
+                    cols = slice(h * N_MOVE, (h + 1) * N_MOVE)
+                    nc.vector.scalar_tensor_tensor(
+                        out=res[:, cols],
+                        in0=acc_tiles[(i, c, h)][:],
+                        scalar=weight(i, c),
+                        in1=res[:, cols],
+                        op0=MULT,
+                        op1=ADD,
+                    )
+            nc.sync.dma_start(out=out_rows[:, i, :], in_=res[:])
+
+        with tc.manual_schedule():
+            for step in range(TILES + 3):
+                if step < TILES:
+                    mix_bias(step)
+                if 0 <= step - 1 < TILES:
+                    transpose_tokens(step - 1)
+                if 0 <= step - 2 < TILES:
+                    quantise_tokens(step - 2)
+                    multiply(step - 2)
+                if 0 <= step - 3:
+                    combine(step - 3)

@@ -27,6 +27,10 @@ CHUNK = 4
 FLOPS = 2 * B * C * L * K * E
 
 
+def by_tensor(i):
+    return i % 4 != 3
+
+
 def tile_model_pa_t_kernel(tc, attn_ctx, Wo, bo, cluster_probs, out):
     nc = tc.nc
 
@@ -41,11 +45,15 @@ def tile_model_pa_t_kernel(tc, attn_ctx, Wo, bo, cluster_probs, out):
         work = ctx.enter_context(tc.tile_pool(name="work", bufs=2))
         res_pool = ctx.enter_context(tc.tile_pool(name="res_pool", bufs=6))
         xt_psum = ctx.enter_context(tc.psum_pool(name="xt_psum", bufs=2))
-        acc_psum = ctx.enter_context(tc.psum_pool(name="acc_psum", bufs=6))
+        bias_psum = ctx.enter_context(tc.psum_pool(name="bias_psum", bufs=2))
+        acc_psum = ctx.enter_context(tc.psum_pool(name="acc_psum", bufs=4))
 
         prob_bf = const.tile([P, TILES * C], BF16)
         nc.scalar.dma_start(out=prob_bf[:], in_=prob_rows)
         bias_all = const.tile([P, C * E], BF16)
+        bias_rows = const.tile([P, E], BF16)
+        nc.scalar.dma_start(out=bias_rows[0:TILES, :], in_=bo[0].partition_broadcast(TILES))
+        nc.scalar.dma_start(out=bias_rows[TILES:P, :], in_=bo[1].partition_broadcast(P - TILES))
         nc.scalar.dma_start(out=bias_all[:], in_=bo.rearrange("c e -> (c e)").partition_broadcast(P))
 
         wo_raw = {}
@@ -74,8 +82,28 @@ def tile_model_pa_t_kernel(tc, attn_ctx, Wo, bo, cluster_probs, out):
 
         ident = const.tile([P, P], F32)
         make_identity(nc, ident[:])
-        prob = const.tile([P, TILES * C], F32)
-        nc.vector.tensor_copy(out=prob[:], in_=prob_bf[:])
+        prob = const.tile([P, P], F32)
+        nc.vector.memset(prob[:, C * TILES : P], 0.0)
+        nc.vector.tensor_copy(
+            out=prob[:, 0 : C * TILES].rearrange("p (c i) -> p c i", c=C),
+            in_=prob_bf[:].rearrange("p (i c) -> p c i", c=C),
+        )
+        select = const.tile([P, TILES], F32)
+        nc.vector.tensor_tensor(out=select[:], in0=ident[:, 0:TILES], in1=ident[:, TILES : 2 * TILES], op=ADD)
+        prob_t_bank = bias_psum.tile([P, P], F32, name="bias_bank")
+        nc.tensor.transpose(prob_t_bank[:], prob[:], ident[:])
+        prob_t = const.tile([P, P], BF16)
+        nc.vector.tensor_copy(out=prob_t[:], in_=prob_t_bank[:])
+        prob_sel = const.tile([P, TILES * P], BF16)
+        for i in range(TILES):
+            if by_tensor(i):
+                nc.vector.tensor_scalar(
+                    out=prob_sel[:, i * P : (i + 1) * P],
+                    in0=prob_t[:],
+                    scalar1=select[:, i : i + 1],
+                    scalar2=None,
+                    op0=MULT,
+                )
 
         wo_codes = {}
         wo_scales = {}
@@ -97,9 +125,23 @@ def tile_model_pa_t_kernel(tc, attn_ctx, Wo, bo, cluster_probs, out):
         acc_tiles = {}
 
         def weight(i, c):
-            return prob[:, C * i + c : C * i + c + 1]
+            return prob[:, TILES * c + i : TILES * c + i + 1]
 
         def mix_bias(i):
+            if by_tensor(i):
+                res = res_pool.tile([P, E], F32)
+                for h in range(HALVES):
+                    bias_bank = bias_psum.tile([P, N_MOVE], F32)
+                    nc.tensor.matmul(
+                        bias_bank[:],
+                        lhsT=prob_sel[:, i * P : (i + 1) * P],
+                        rhs=bias_rows[:, h * N_MOVE : (h + 1) * N_MOVE],
+                        start=True,
+                        stop=True,
+                    )
+                    nc.scalar.copy(out=res[:, h * N_MOVE : (h + 1) * N_MOVE], in_=bias_bank[:])
+                res_tiles[i] = res
+                return
             scaled = work.tile([P, C * E], F32)
             for c in range(C):
                 nc.scalar.activation(
@@ -166,10 +208,10 @@ def tile_model_pa_t_kernel(tc, attn_ctx, Wo, bo, cluster_probs, out):
 
         with tc.manual_schedule():
             for step in range(TILES + 3):
-                if step < TILES:
-                    mix_bias(step)
                 if 0 <= step - 1 < TILES:
                     transpose_tokens(step - 1)
+                if step < TILES:
+                    mix_bias(step)
                 if 0 <= step - 2 < TILES:
                     quantise_tokens(step - 2)
                     multiply(step - 2)

@@ -43,10 +43,11 @@ def tile_model_pa_t_kernel(tc, attn_ctx, Wo, bo, cluster_probs, out):
         const = ctx.enter_context(tc.tile_pool(name="const", bufs=1))
         x_pool = ctx.enter_context(tc.tile_pool(name="x_pool", bufs=TILES // CHUNK))
         work = ctx.enter_context(tc.tile_pool(name="work", bufs=2))
-        res_pool = ctx.enter_context(tc.tile_pool(name="res_pool", bufs=6))
-        xt_psum = ctx.enter_context(tc.psum_pool(name="xt_psum", bufs=2))
-        bias_psum = ctx.enter_context(tc.psum_pool(name="bias_psum", bufs=2))
-        acc_psum = ctx.enter_context(tc.psum_pool(name="acc_psum", bufs=4))
+        part_pool = ctx.enter_context(tc.tile_pool(name="part_pool", bufs=3))
+        res_pool = ctx.enter_context(tc.tile_pool(name="res_pool", bufs=8))
+        xt_psum = ctx.enter_context(tc.psum_pool(name="xt_psum", bufs=1))
+        bias_psum = ctx.enter_context(tc.psum_pool(name="bias_psum", bufs=1))
+        acc_psum = ctx.enter_context(tc.psum_pool(name="acc_psum", bufs=6))
 
         prob_bf = const.tile([P, TILES * C], BF16)
         nc.scalar.dma_start(out=prob_bf[:], in_=prob_rows)
@@ -123,36 +124,37 @@ def tile_model_pa_t_kernel(tc, attn_ctx, Wo, bo, cluster_probs, out):
         grouped_tiles = {}
         code_tiles = {}
         acc_tiles = {}
+        part_tiles = {}
 
         def weight(i, c):
             return prob[:, TILES * c + i : TILES * c + i + 1]
 
+        def bias_half(i, h):
+            cols = slice(h * N_MOVE, (h + 1) * N_MOVE)
+            bias_bank = bias_psum.tile([P, N_MOVE], F32)
+            nc.tensor.matmul(
+                bias_bank[:],
+                lhsT=prob_sel[:, i * P : (i + 1) * P],
+                rhs=bias_rows[:, cols],
+                start=True,
+                stop=True,
+            )
+            nc.scalar.copy(out=res_tiles[i][:, cols], in_=bias_bank[:])
+
         def mix_bias(i):
-            if by_tensor(i):
-                res = res_pool.tile([P, E], F32)
-                for h in range(HALVES):
-                    bias_bank = bias_psum.tile([P, N_MOVE], F32)
-                    nc.tensor.matmul(
-                        bias_bank[:],
-                        lhsT=prob_sel[:, i * P : (i + 1) * P],
-                        rhs=bias_rows[:, h * N_MOVE : (h + 1) * N_MOVE],
-                        start=True,
-                        stop=True,
-                    )
-                    nc.scalar.copy(out=res[:, h * N_MOVE : (h + 1) * N_MOVE], in_=bias_bank[:])
-                res_tiles[i] = res
-                return
             scaled = work.tile([P, C * E], F32)
-            for c in range(C):
-                nc.scalar.activation(
-                    out=scaled[:, c * E : (c + 1) * E],
-                    in_=bias_all[:, c * E : (c + 1) * E],
-                    func=COPY,
-                    scale=weight(i, c),
-                )
-            res = res_pool.tile([P, E], F32)
-            nc.gpsimd.tensor_tensor(out=res[:], in0=scaled[:, 0:E], in1=scaled[:, E : 2 * E], op=ADD)
-            res_tiles[i] = res
+            nc.scalar.activation(out=scaled[:, 0:E], in_=bias_all[:, 0:E], func=COPY, scale=weight(i, 0))
+            nc.gpsimd.tensor_scalar(
+                out=scaled[:, E : 2 * E],
+                in0=bias_all[:, E : 2 * E],
+                scalar1=weight(i, 1),
+                scalar2=0.0,
+                op0=MULT,
+                op1=ADD,
+            )
+            nc.gpsimd.tensor_tensor(
+                out=res_tiles[i][:], in0=scaled[:, 0:E], in1=scaled[:, E : 2 * E], op=ADD
+            )
 
         def transpose_tokens(i):
             x_words = x_chunks[i // CHUNK][:].bitcast(F32)
@@ -175,45 +177,61 @@ def tile_model_pa_t_kernel(tc, attn_ctx, Wo, bo, cluster_probs, out):
             nc.vector.quantize_mx(out=codes[:].bitcast(FP8X4), scales=scales[:], in_=grouped_tiles[i][:])
             code_tiles[i] = (codes, scales)
 
-        def multiply(i):
+        def multiply(i, c, h):
             codes, scales = code_tiles[i]
-            for c in range(C):
-                for h in range(HALVES):
-                    acc = acc_psum.tile([P, N_MOVE], F32)
-                    nc.tensor.matmul_mx(
-                        out=acc[:],
-                        lhsT=codes[:, c * P : (c + 1) * P].bitcast(FP8X4),
-                        lhsT_scale=scales[:, c * P : (c + 1) * P],
-                        rhs=wo_codes[c][:, h * N_MOVE : (h + 1) * N_MOVE].bitcast(FP8X4),
-                        rhs_scale=wo_scales[c][:, h * N_MOVE : (h + 1) * N_MOVE],
-                        start=True,
-                        stop=True,
-                    )
-                    acc_tiles[(i, c, h)] = acc
+            acc = acc_psum.tile([P, N_MOVE], F32)
+            nc.tensor.matmul_mx(
+                out=acc[:],
+                lhsT=codes[:, c * P : (c + 1) * P].bitcast(FP8X4),
+                lhsT_scale=scales[:, c * P : (c + 1) * P],
+                rhs=wo_codes[c][:, h * N_MOVE : (h + 1) * N_MOVE].bitcast(FP8X4),
+                rhs_scale=wo_scales[c][:, h * N_MOVE : (h + 1) * N_MOVE],
+                start=True,
+                stop=True,
+            )
+            acc_tiles[(i, c, h)] = acc
 
-        def combine(i):
-            res = res_tiles[i]
-            for c in range(C):
-                for h in range(HALVES):
-                    cols = slice(h * N_MOVE, (h + 1) * N_MOVE)
-                    nc.vector.scalar_tensor_tensor(
-                        out=res[:, cols],
-                        in0=acc_tiles[(i, c, h)][:],
-                        scalar=weight(i, c),
-                        in1=res[:, cols],
-                        op0=MULT,
-                        op1=ADD,
-                    )
-            nc.sync.dma_start(out=out_rows[:, i, :], in_=res[:])
+        def weigh_part(i):
+            part = part_pool.tile([P, N_MOVE], F32)
+            nc.scalar.activation(out=part[:], in_=acc_tiles[(i, 0, 0)][:], func=COPY, scale=weight(i, 0))
+            part_tiles[i] = part
+
+        def combine(i, c, h):
+            half = res_tiles[i][:, h * N_MOVE : (h + 1) * N_MOVE]
+            nc.vector.scalar_tensor_tensor(
+                out=half, in0=acc_tiles[(i, c, h)][:], scalar=weight(i, c), in1=half, op0=MULT, op1=ADD
+            )
+
+        def finish(i):
+            left = res_tiles[i][:, 0:N_MOVE]
+            nc.gpsimd.tensor_tensor(out=left, in0=part_tiles[i][:], in1=left, op=ADD)
+            nc.sync.dma_start(out=out_rows[:, i, :], in_=res_tiles[i][:])
 
         with tc.manual_schedule():
             for step in range(TILES + 3):
-                if 0 <= step - 1 < TILES:
-                    transpose_tokens(step - 1)
-                if step < TILES:
-                    mix_bias(step)
-                if 0 <= step - 2 < TILES:
-                    quantise_tokens(step - 2)
-                    multiply(step - 2)
-                if 0 <= step - 3:
-                    combine(step - 3)
+                new, turned, product, done = step, step - 1, step - 2, step - 3
+                if new < TILES:
+                    res_tiles[new] = res_pool.tile([P, E], F32, name="res")
+                    if not by_tensor(new):
+                        mix_bias(new)
+                if 0 <= turned < TILES:
+                    transpose_tokens(turned)
+                if 0 <= product < TILES:
+                    multiply(product, 0, 0)
+                    weigh_part(product)
+                if new < TILES and by_tensor(new):
+                    bias_half(new, 0)
+                if 0 <= product < TILES:
+                    multiply(product, 0, 1)
+                    multiply(product, 1, 0)
+                    multiply(product, 1, 1)
+                if new < TILES and by_tensor(new):
+                    bias_half(new, 1)
+                if 0 <= done:
+                    combine(done, 0, 1)
+                    combine(done, 1, 0)
+                if 0 <= turned < TILES:
+                    quantise_tokens(turned)
+                if 0 <= done:
+                    combine(done, 1, 1)
+                    finish(done)

@@ -23,7 +23,7 @@ WORDS = K // 2
 N_MOVE = 512
 HALVES = E // N_MOVE
 TILES = B * L // P
-CHUNK = 4
+CHUNKS = (2, 2, 4, 4, 4, 4, 4, 4, 4)
 FLOPS = 2 * B * C * L * K * E
 
 
@@ -41,24 +41,20 @@ def tile_model_pa_t_kernel(tc, attn_ctx, Wo, bo, cluster_probs, out):
 
     with ExitStack() as ctx:
         const = ctx.enter_context(tc.tile_pool(name="const", bufs=1))
-        x_pool = ctx.enter_context(tc.tile_pool(name="x_pool", bufs=TILES // CHUNK))
-        work = ctx.enter_context(tc.tile_pool(name="work", bufs=2))
-        part_pool = ctx.enter_context(tc.tile_pool(name="part_pool", bufs=3))
-        res_pool = ctx.enter_context(tc.tile_pool(name="res_pool", bufs=8))
-        xt_psum = ctx.enter_context(tc.psum_pool(name="xt_psum", bufs=1))
-        bias_psum = ctx.enter_context(tc.psum_pool(name="bias_psum", bufs=1))
-        acc_psum = ctx.enter_context(tc.psum_pool(name="acc_psum", bufs=6))
+        work = ctx.enter_context(tc.tile_pool(name="work", bufs=3))
+        res_pool = ctx.enter_context(tc.tile_pool(name="res_pool", bufs=9))
+        banks = ctx.enter_context(tc.psum_pool(name="banks", bufs=8))
+        ctx.enter_context(tc.manual_schedule())
 
         prob_bf = const.tile([P, TILES * C], BF16)
         nc.scalar.dma_start(out=prob_bf[:], in_=prob_rows)
-        bias_all = const.tile([P, C * E], BF16)
-        bias_rows = const.tile([P, E], BF16)
-        nc.scalar.dma_start(out=bias_rows[0:TILES, :], in_=bo[0].partition_broadcast(TILES))
-        nc.scalar.dma_start(out=bias_rows[TILES:P, :], in_=bo[1].partition_broadcast(P - TILES))
-        nc.scalar.dma_start(out=bias_all[:], in_=bo.rearrange("c e -> (c e)").partition_broadcast(P))
+        bo_pad = const.tile([P, E], BF16)
+        nc.vector.memset(bo_pad[:].bitcast(U32), 0)
+        nc.scalar.dma_start(out=bo_pad[0:1, :], in_=bo[0:1, :])
+        nc.scalar.dma_start(out=bo_pad[TILES : TILES + 1, :], in_=bo[1:2, :])
 
         wo_raw = {}
-        x_chunks = {}
+        x_tiles = {}
 
         def load_wo(c):
             raw = const.tile([P, PACK * E], BF16, name="wo_raw%d" % c)
@@ -69,56 +65,81 @@ def tile_model_pa_t_kernel(tc, attn_ctx, Wo, bo, cluster_probs, out):
             wo_raw[c] = raw
 
         def load_x(g):
-            x = x_pool.tile([P, 2 * CHUNK * K], BF16)
+            first, size = sum(CHUNKS[:g]), CHUNKS[g]
+            x = const.tile([P, 2 * size * K], BF16, name="x%d" % g)
             nc.sync.dma_start(
                 out=x[:].rearrange("p (j f) -> p j f", j=2),
-                in_=attn_rows[:, :, g * CHUNK * K : (g + 1) * CHUNK * K],
+                in_=attn_rows[:, :, first * K : (first + size) * K],
             )
-            x_chunks[g] = x
+            for n in range(size):
+                x_tiles[first + n] = (x, n, size)
 
         load_wo(0)
+        load_x(0)
         load_wo(1)
-        for g in range(TILES // CHUNK):
+        load_x(1)
+        bias_all = const.tile([P, C * E], BF16)
+        nc.sync.dma_start(out=bias_all[:], in_=bo.rearrange("c e -> (c e)").partition_broadcast(P))
+        for g in range(2, len(CHUNKS)):
             load_x(g)
 
         ident = const.tile([P, P], F32)
         make_identity(nc, ident[:])
         prob = const.tile([P, P], F32)
         nc.vector.memset(prob[:, C * TILES : P], 0.0)
+        select = const.tile([P, TILES], F32)
+        nc.vector.tensor_tensor(out=select[:], in0=ident[:, 0:TILES], in1=ident[:, TILES : 2 * TILES], op=ADD)
+        spread = const.tile([P, P], BF16)
+        nc.vector.tensor_copy(out=spread[:, 0:TILES], in_=ident[:, 0:1].to_broadcast([P, TILES]))
+        nc.vector.tensor_copy(out=spread[:, TILES:P], in_=ident[:, TILES : TILES + 1].to_broadcast([P, P - TILES]))
         nc.vector.tensor_copy(
             out=prob[:, 0 : C * TILES].rearrange("p (c i) -> p c i", c=C),
             in_=prob_bf[:].rearrange("p (i c) -> p c i", c=C),
         )
-        select = const.tile([P, TILES], F32)
-        nc.vector.tensor_tensor(out=select[:], in0=ident[:, 0:TILES], in1=ident[:, TILES : 2 * TILES], op=ADD)
-        prob_t_bank = bias_psum.tile([P, P], F32, name="bias_bank")
+        prob_t_bank = banks.tile([P, P], F32, name="bank")
         nc.tensor.transpose(prob_t_bank[:], prob[:], ident[:])
         prob_t = const.tile([P, P], BF16)
         nc.vector.tensor_copy(out=prob_t[:], in_=prob_t_bank[:])
+        bias_rows = const.tile([P, E], BF16)
+        for h in range(HALVES):
+            cols = slice(h * N_MOVE, (h + 1) * N_MOVE)
+            bank = banks.tile([P, N_MOVE], F32)
+            nc.tensor.matmul(bank[:], lhsT=spread[:], rhs=bo_pad[:, cols], start=True, stop=True)
+            nc.scalar.copy(out=bias_rows[:, cols], in_=bank[:])
         prob_sel = const.tile([P, TILES * P], BF16)
-        for i in range(TILES):
-            if by_tensor(i):
-                nc.vector.tensor_scalar(
-                    out=prob_sel[:, i * P : (i + 1) * P],
-                    in0=prob_t[:],
-                    scalar1=select[:, i : i + 1],
-                    scalar2=None,
-                    op0=MULT,
-                )
 
-        wo_codes = {}
-        wo_scales = {}
-        for c in range(C):
-            grouped_w = const.tile([P, E * PACK], BF16, name="wo_grouped%d" % c, align_bytes=64)
-            nc.vector.tensor_copy(
-                out=grouped_w[:].rearrange("p (n i t) -> p n t i", i=4, t=PACK),
-                in_=wo_raw[c][:].rearrange("p (t n i) -> p n t i", t=PACK, i=4),
+        def select_rows(i):
+            nc.vector.tensor_scalar(
+                out=prob_sel[:, i * P : (i + 1) * P],
+                in0=prob_t[:],
+                scalar1=select[:, i : i + 1],
+                scalar2=None,
+                op0=MULT,
             )
-            codes_w = const.tile([P, E], U32, name="wo_codes%d" % c, align_bytes=64)
-            scales_w = const.tile([P, E], U8, name="wo_scales%d" % c, align_bytes=64)
-            nc.vector.quantize_mx(out=codes_w[:].bitcast(FP8X4), scales=scales_w[:], in_=grouped_w[:])
-            wo_codes[c] = codes_w
-            wo_scales[c] = scales_w
+
+        wo_grouped = []
+        wo_codes = []
+        wo_scales = []
+        for c in range(C):
+            wo_grouped.append(const.tile([P, E * PACK], BF16, name="wo_grouped%d" % c, align_bytes=64))
+            wo_codes.append(const.tile([P, E], U32, name="wo_codes%d" % c, align_bytes=64))
+            wo_scales.append(const.tile([P, E], U8, name="wo_scales%d" % c, align_bytes=64))
+
+        def group_wo(copy, c, h):
+            copy(
+                out=wo_grouped[c][:, h * N_MOVE * PACK : (h + 1) * N_MOVE * PACK].rearrange(
+                    "p (n i t) -> p n t i", i=4, t=PACK
+                ),
+                in_=wo_raw[c][:].rearrange("p (t h n i) -> p h n t i", t=PACK, h=HALVES, i=4)[:, h],
+            )
+
+        def quantise_wo(c, h):
+            cols = slice(h * N_MOVE, (h + 1) * N_MOVE)
+            nc.vector.quantize_mx(
+                out=wo_codes[c][:, cols].bitcast(FP8X4),
+                scales=wo_scales[c][:, cols],
+                in_=wo_grouped[c][:, h * N_MOVE * PACK : (h + 1) * N_MOVE * PACK],
+            )
 
         res_tiles = {}
         grouped_tiles = {}
@@ -131,15 +152,11 @@ def tile_model_pa_t_kernel(tc, attn_ctx, Wo, bo, cluster_probs, out):
 
         def bias_half(i, h):
             cols = slice(h * N_MOVE, (h + 1) * N_MOVE)
-            bias_bank = bias_psum.tile([P, N_MOVE], F32)
+            bank = banks.tile([P, N_MOVE], F32)
             nc.tensor.matmul(
-                bias_bank[:],
-                lhsT=prob_sel[:, i * P : (i + 1) * P],
-                rhs=bias_rows[:, cols],
-                start=True,
-                stop=True,
+                bank[:], lhsT=prob_sel[:, i * P : (i + 1) * P], rhs=bias_rows[:, cols], start=True, stop=True
             )
-            nc.scalar.copy(out=res_tiles[i][:, cols], in_=bias_bank[:])
+            nc.scalar.copy(out=res_tiles[i][:, cols], in_=bank[:])
 
         def mix_bias(i):
             scaled = work.tile([P, C * E], F32)
@@ -152,22 +169,21 @@ def tile_model_pa_t_kernel(tc, attn_ctx, Wo, bo, cluster_probs, out):
                 op0=MULT,
                 op1=ADD,
             )
-            nc.gpsimd.tensor_tensor(
-                out=res_tiles[i][:], in0=scaled[:, 0:E], in1=scaled[:, E : 2 * E], op=ADD
-            )
+            nc.gpsimd.tensor_tensor(out=res_tiles[i][:], in0=scaled[:, 0:E], in1=scaled[:, E : 2 * E], op=ADD)
 
         def transpose_tokens(i):
-            x_words = x_chunks[i // CHUNK][:].bitcast(F32)
-            xt = xt_psum.tile([P, PACK * P], F32)
+            x, n, size = x_tiles[i]
+            x_words = x[:].bitcast(F32)
+            bank = banks.tile([P, PACK * P], F32)
             for j in range(2):
                 for u in range(2):
                     s = 2 * j + u
-                    first = (j * CHUNK + i % CHUNK) * WORDS + u * P
-                    nc.tensor.transpose(xt[:, s * P : (s + 1) * P], x_words[:, first : first + P], ident[:])
+                    first = (j * size + n) * WORDS + u * P
+                    nc.tensor.transpose(bank[:, s * P : (s + 1) * P], x_words[:, first : first + P], ident[:])
             grouped = work.tile([P, C * P * PACK], BF16, align_bytes=64)
             nc.scalar.copy(
                 out=grouped[:].bitcast(F32).rearrange("p (c b s) -> p c b s", c=C, s=PACK),
-                in_=xt[:].rearrange("p (s b c) -> p c b s", s=PACK, c=C),
+                in_=bank[:].rearrange("p (s b c) -> p c b s", s=PACK, c=C),
             )
             grouped_tiles[i] = grouped
 
@@ -179,9 +195,9 @@ def tile_model_pa_t_kernel(tc, attn_ctx, Wo, bo, cluster_probs, out):
 
         def multiply(i, c, h):
             codes, scales = code_tiles[i]
-            acc = acc_psum.tile([P, N_MOVE], F32)
+            bank = banks.tile([P, N_MOVE], F32)
             nc.tensor.matmul_mx(
-                out=acc[:],
+                out=bank[:],
                 lhsT=codes[:, c * P : (c + 1) * P].bitcast(FP8X4),
                 lhsT_scale=scales[:, c * P : (c + 1) * P],
                 rhs=wo_codes[c][:, h * N_MOVE : (h + 1) * N_MOVE].bitcast(FP8X4),
@@ -189,10 +205,10 @@ def tile_model_pa_t_kernel(tc, attn_ctx, Wo, bo, cluster_probs, out):
                 start=True,
                 stop=True,
             )
-            acc_tiles[(i, c, h)] = acc
+            acc_tiles[(i, c, h)] = bank
 
         def weigh_part(i):
-            part = part_pool.tile([P, N_MOVE], F32)
+            part = work.tile([P, N_MOVE], F32)
             nc.scalar.activation(out=part[:], in_=acc_tiles[(i, 0, 0)][:], func=COPY, scale=weight(i, 0))
             part_tiles[i] = part
 
@@ -207,31 +223,50 @@ def tile_model_pa_t_kernel(tc, attn_ctx, Wo, bo, cluster_probs, out):
             nc.gpsimd.tensor_tensor(out=left, in0=part_tiles[i][:], in1=left, op=ADD)
             nc.sync.dma_start(out=out_rows[:, i, :], in_=res_tiles[i][:])
 
-        with tc.manual_schedule():
-            for step in range(TILES + 3):
-                new, turned, product, done = step, step - 1, step - 2, step - 3
-                if new < TILES:
-                    res_tiles[new] = res_pool.tile([P, E], F32, name="res")
-                    if not by_tensor(new):
-                        mix_bias(new)
-                if 0 <= turned < TILES:
-                    transpose_tokens(turned)
-                if 0 <= product < TILES:
-                    multiply(product, 0, 0)
-                    weigh_part(product)
-                if new < TILES and by_tensor(new):
-                    bias_half(new, 0)
-                if 0 <= product < TILES:
-                    multiply(product, 0, 1)
-                    multiply(product, 1, 0)
-                    multiply(product, 1, 1)
-                if new < TILES and by_tensor(new):
-                    bias_half(new, 1)
-                if 0 <= done:
-                    combine(done, 0, 1)
-                    combine(done, 1, 0)
-                if 0 <= turned < TILES:
-                    quantise_tokens(turned)
-                if 0 <= done:
-                    combine(done, 1, 1)
-                    finish(done)
+        tensor_tiles = [i for i in range(TILES) if by_tensor(i)]
+        for i in tensor_tiles[:8]:
+            select_rows(i)
+        group_wo(nc.vector.tensor_copy, 0, 0)
+        group_wo(nc.vector.tensor_copy, 0, 1)
+        quantise_wo(0, 0)
+        quantise_wo(0, 1)
+        transpose_tokens(0)
+        transpose_tokens(1)
+        group_wo(nc.vector.tensor_copy, 1, 0)
+        quantise_tokens(0)
+        quantise_wo(1, 0)
+        group_wo(nc.vector.tensor_copy, 1, 1)
+        for i in tensor_tiles[8:]:
+            select_rows(i)
+        quantise_wo(1, 1)
+
+        def make_res(i):
+            res_tiles[i] = res_pool.tile([P, E], F32, name="res")
+
+        for step in range(-3, TILES + 1):
+            mixed, bias, turned, quant, prod, done = step + 3, step + 1, step + 2, step + 1, step, step - 1
+            if mixed < TILES:
+                make_res(mixed)
+                if not by_tensor(mixed):
+                    mix_bias(mixed)
+            if 2 <= turned < TILES:
+                transpose_tokens(turned)
+            if 0 <= bias < TILES and by_tensor(bias):
+                bias_half(bias, 1)
+            if 0 <= prod < TILES:
+                multiply(prod, 0, 1)
+                combine(prod, 0, 1)
+            if 0 <= bias < TILES and by_tensor(bias):
+                bias_half(bias, 0)
+            if 0 <= prod < TILES:
+                multiply(prod, 1, 0)
+                combine(prod, 1, 0)
+                multiply(prod, 0, 0)
+                weigh_part(prod)
+            if 1 <= quant < TILES:
+                quantise_tokens(quant)
+            if 0 <= prod < TILES:
+                multiply(prod, 1, 1)
+                combine(prod, 1, 1)
+            if 0 <= done:
+                finish(done)

@@ -27,8 +27,12 @@ CHUNKS = (2, 2, 4, 4, 4, 4, 4, 4, 4)
 FLOPS = 2 * B * C * L * K * E
 
 
+def kind(i):
+    return "split" if i % 4 == 1 else "plain" if i == TILES - 1 else "shared"
+
+
 def by_tensor(i):
-    return i % 4 != 3
+    return kind(i) != "split"
 
 
 def tile_model_pa_t_kernel(tc, attn_ctx, Wo, bo, cluster_probs, out):
@@ -41,7 +45,7 @@ def tile_model_pa_t_kernel(tc, attn_ctx, Wo, bo, cluster_probs, out):
 
     with ExitStack() as ctx:
         const = ctx.enter_context(tc.tile_pool(name="const", bufs=1))
-        work = ctx.enter_context(tc.tile_pool(name="work", bufs=3))
+        work = ctx.enter_context(tc.tile_pool(name="work", bufs=5))
         res_pool = ctx.enter_context(tc.tile_pool(name="res_pool", bufs=9))
         banks = ctx.enter_context(tc.psum_pool(name="banks", bufs=8))
         ctx.enter_context(tc.manual_schedule())
@@ -158,18 +162,12 @@ def tile_model_pa_t_kernel(tc, attn_ctx, Wo, bo, cluster_probs, out):
             )
             nc.scalar.copy(out=res_tiles[i][:, cols], in_=bank[:])
 
-        def mix_bias(i):
-            scaled = work.tile([P, C * E], F32)
-            nc.scalar.activation(out=scaled[:, 0:E], in_=bias_all[:, 0:E], func=COPY, scale=weight(i, 0))
-            nc.gpsimd.tensor_scalar(
-                out=scaled[:, E : 2 * E],
-                in0=bias_all[:, E : 2 * E],
-                scalar1=weight(i, 1),
-                scalar2=0.0,
-                op0=MULT,
-                op1=ADD,
-            )
-            nc.gpsimd.tensor_tensor(out=res_tiles[i][:], in0=scaled[:, 0:E], in1=scaled[:, E : 2 * E], op=ADD)
+        def scale_bias(i):
+            part_tiles[i] = work.tile([P, E], F32, name="part")
+            for c, row in ((0, res_tiles[i]), (1, part_tiles[i])):
+                nc.scalar.activation(
+                    out=row[:], in_=bias_all[:, c * E : (c + 1) * E], func=COPY, scale=weight(i, c)
+                )
 
         def transpose_tokens(i):
             x, n, size = x_tiles[i]
@@ -208,9 +206,10 @@ def tile_model_pa_t_kernel(tc, attn_ctx, Wo, bo, cluster_probs, out):
             acc_tiles[(i, c, h)] = bank
 
         def weigh_part(i):
-            part = work.tile([P, N_MOVE], F32)
-            nc.scalar.activation(out=part[:], in_=acc_tiles[(i, 0, 0)][:], func=COPY, scale=weight(i, 0))
-            part_tiles[i] = part
+            part_tiles[i] = work.tile([P, E], F32, name="part")
+            nc.scalar.activation(
+                out=part_tiles[i][:, 0:N_MOVE], in_=acc_tiles[(i, 0, 0)][:], func=COPY, scale=weight(i, 0)
+            )
 
         def combine(i, c, h):
             half = res_tiles[i][:, h * N_MOVE : (h + 1) * N_MOVE]
@@ -219,8 +218,11 @@ def tile_model_pa_t_kernel(tc, attn_ctx, Wo, bo, cluster_probs, out):
             )
 
         def finish(i):
-            left = res_tiles[i][:, 0:N_MOVE]
-            nc.gpsimd.tensor_tensor(out=left, in0=part_tiles[i][:], in1=left, op=ADD)
+            width = {"split": E, "shared": N_MOVE, "plain": 0}[kind(i)]
+            if width:
+                nc.gpsimd.tensor_tensor(
+                    out=res_tiles[i][:, 0:width], in0=part_tiles[i][:, 0:width], in1=res_tiles[i][:, 0:width], op=ADD
+                )
             nc.sync.dma_start(out=out_rows[:, i, :], in_=res_tiles[i][:])
 
         tensor_tiles = [i for i in range(TILES) if by_tensor(i)]
@@ -243,30 +245,32 @@ def tile_model_pa_t_kernel(tc, attn_ctx, Wo, bo, cluster_probs, out):
         def make_res(i):
             res_tiles[i] = res_pool.tile([P, E], F32, name="res")
 
-        for step in range(-3, TILES + 1):
-            mixed, bias, turned, quant, prod, done = step + 3, step + 1, step + 2, step + 1, step, step - 1
-            if mixed < TILES:
-                make_res(mixed)
-                if not by_tensor(mixed):
-                    mix_bias(mixed)
+        for step in range(-1, TILES + 1):
+            bias, turned, quant, prod, done = step + 1, step + 3, step + 2, step, step - 1
             if 2 <= turned < TILES:
                 transpose_tokens(turned)
-            if 0 <= bias < TILES and by_tensor(bias):
-                bias_half(bias, 1)
+            if 0 <= bias < TILES:
+                make_res(bias)
+                if by_tensor(bias):
+                    bias_half(bias, 1)
+                else:
+                    scale_bias(bias)
             if 0 <= prod < TILES:
                 multiply(prod, 0, 1)
                 combine(prod, 0, 1)
+                multiply(prod, 0, 0)
+                if kind(prod) == "shared":
+                    weigh_part(prod)
+                else:
+                    combine(prod, 0, 0)
             if 0 <= bias < TILES and by_tensor(bias):
                 bias_half(bias, 0)
             if 0 <= prod < TILES:
-                multiply(prod, 1, 0)
-                combine(prod, 1, 0)
-                multiply(prod, 0, 0)
-                weigh_part(prod)
-            if 1 <= quant < TILES:
-                quantise_tokens(quant)
-            if 0 <= prod < TILES:
                 multiply(prod, 1, 1)
                 combine(prod, 1, 1)
+                multiply(prod, 1, 0)
+                combine(prod, 1, 0)
+            if 1 <= quant < TILES:
+                quantise_tokens(quant)
             if 0 <= done:
                 finish(done)

@@ -23,17 +23,14 @@ WORDS = K // 2
 N_MOVE = 512
 HALVES = E // N_MOVE
 TILES = B * L // P
+BO_ROW = 32
+WEIGHT_RUN = 8
 CHUNKS = (2, 2, 4, 4, 4, 4, 4, 4, 4)
 FLOPS = 2 * B * C * L * K * E
 
 
 def kind(i):
-    return "split" if i % 4 == 1 else "plain" if i == TILES - 1 else "shared"
-
-
-def by_tensor(i):
-    return kind(i) != "split"
-
+    return "plain" if i == TILES - 1 else "split" if i % 4 == 1 else "shared"
 
 def tile_model_pa_t_kernel(tc, attn_ctx, Wo, bo, cluster_probs, out):
     nc = tc.nc
@@ -45,7 +42,8 @@ def tile_model_pa_t_kernel(tc, attn_ctx, Wo, bo, cluster_probs, out):
 
     with ExitStack() as ctx:
         const = ctx.enter_context(tc.tile_pool(name="const", bufs=1))
-        work = ctx.enter_context(tc.tile_pool(name="work", bufs=5))
+        work = ctx.enter_context(tc.tile_pool(name="work", bufs=4))
+        part_pool = ctx.enter_context(tc.tile_pool(name="part_pool", bufs=5))
         res_pool = ctx.enter_context(tc.tile_pool(name="res_pool", bufs=9))
         banks = ctx.enter_context(tc.psum_pool(name="banks", bufs=8))
         ctx.enter_context(tc.manual_schedule())
@@ -54,19 +52,23 @@ def tile_model_pa_t_kernel(tc, attn_ctx, Wo, bo, cluster_probs, out):
         nc.scalar.dma_start(out=prob_bf[:], in_=prob_rows)
         bo_pad = const.tile([P, E], BF16)
         nc.vector.memset(bo_pad[:].bitcast(U32), 0)
-        nc.scalar.dma_start(out=bo_pad[0:1, :], in_=bo[0:1, :])
-        nc.scalar.dma_start(out=bo_pad[TILES : TILES + 1, :], in_=bo[1:2, :])
+        for c in range(C):
+            nc.scalar.dma_start(out=bo_pad[c * BO_ROW : c * BO_ROW + 1, :], in_=bo[c : c + 1, :])
+        prob_wide = const.tile([P, TILES * P], BF16)
+        nc.vector.memset(prob_wide[:].bitcast(U32), 0)
 
         wo_raw = {}
         x_tiles = {}
 
-        def load_wo(c):
-            raw = const.tile([P, PACK * E], BF16, name="wo_raw%d" % c)
-            nc.sync.dma_start(
-                out=raw[:].rearrange("p (u f) -> p u f", u=2),
-                in_=wo_rows[c].rearrange("(u p r) e -> p u (r e)", u=2, r=2),
-            )
-            wo_raw[c] = raw
+        def load_wo(c, h):
+            raw = const.tile([P, PACK * N_MOVE], BF16, name="wo_raw%d%d" % (c, h))
+            for u in range(2):
+                rows = wo_rows[c][2 * P * u : 2 * P * (u + 1), h * N_MOVE : (h + 1) * N_MOVE]
+                nc.sync.dma_start(
+                    out=raw[:, 2 * N_MOVE * u : 2 * N_MOVE * (u + 1)].rearrange("p (r e) -> p r e", r=2),
+                    in_=rows.rearrange("(p r) e -> p r e", r=2),
+                )
+            wo_raw[(c, h)] = raw
 
         def load_x(g):
             first, size = sum(CHUNKS[:g]), CHUNKS[g]
@@ -78,9 +80,11 @@ def tile_model_pa_t_kernel(tc, attn_ctx, Wo, bo, cluster_probs, out):
             for n in range(size):
                 x_tiles[first + n] = (x, n, size)
 
-        load_wo(0)
+        load_wo(0, 0)
+        load_wo(0, 1)
         load_x(0)
-        load_wo(1)
+        load_wo(1, 0)
+        load_wo(1, 1)
         load_x(1)
         bias_all = const.tile([P, C * E], BF16)
         nc.sync.dma_start(out=bias_all[:], in_=bo.rearrange("c e -> (c e)").partition_broadcast(P))
@@ -89,37 +93,22 @@ def tile_model_pa_t_kernel(tc, attn_ctx, Wo, bo, cluster_probs, out):
 
         ident = const.tile([P, P], F32)
         make_identity(nc, ident[:])
-        prob = const.tile([P, P], F32)
-        nc.vector.memset(prob[:, C * TILES : P], 0.0)
-        select = const.tile([P, TILES], F32)
-        nc.vector.tensor_tensor(out=select[:], in0=ident[:, 0:TILES], in1=ident[:, TILES : 2 * TILES], op=ADD)
-        spread = const.tile([P, P], BF16)
-        nc.vector.tensor_copy(out=spread[:, 0:TILES], in_=ident[:, 0:1].to_broadcast([P, TILES]))
-        nc.vector.tensor_copy(out=spread[:, TILES:P], in_=ident[:, TILES : TILES + 1].to_broadcast([P, P - TILES]))
+        ident_bf = const.tile([P, P], BF16)
+        nc.vector.tensor_copy(out=ident_bf[:], in_=ident[:])
+        prob = const.tile([P, TILES * C], F32)
+        nc.vector.tensor_copy(out=prob[:], in_=prob_bf[:])
         nc.vector.tensor_copy(
-            out=prob[:, 0 : C * TILES].rearrange("p (c i) -> p c i", c=C),
-            in_=prob_bf[:].rearrange("p (i c) -> p c i", c=C),
+            out=prob_wide[:].rearrange("p (i w) -> p i w", w=P)[:, :, 0 : C * BO_ROW : BO_ROW],
+            in_=prob_bf[:].rearrange("p (i c) -> p i c", c=C),
         )
-        prob_t_bank = banks.tile([P, P], F32, name="bank")
-        nc.tensor.transpose(prob_t_bank[:], prob[:], ident[:])
-        prob_t = const.tile([P, P], BF16)
-        nc.vector.tensor_copy(out=prob_t[:], in_=prob_t_bank[:])
-        bias_rows = const.tile([P, E], BF16)
-        for h in range(HALVES):
-            cols = slice(h * N_MOVE, (h + 1) * N_MOVE)
-            bank = banks.tile([P, N_MOVE], F32)
-            nc.tensor.matmul(bank[:], lhsT=spread[:], rhs=bo_pad[:, cols], start=True, stop=True)
-            nc.scalar.copy(out=bias_rows[:, cols], in_=bank[:])
-        prob_sel = const.tile([P, TILES * P], BF16)
+        prob_t = const.tile([P, TILES * P], BF16)
 
-        def select_rows(i):
-            nc.vector.tensor_scalar(
-                out=prob_sel[:, i * P : (i + 1) * P],
-                in0=prob_t[:],
-                scalar1=select[:, i : i + 1],
-                scalar2=None,
-                op0=MULT,
-            )
+        def transpose_weights(first):
+            bank = banks.tile([P, WEIGHT_RUN * P], BF16)
+            for n in range(WEIGHT_RUN):
+                i = first + n
+                nc.tensor.transpose(bank[:, n * P : (n + 1) * P], prob_wide[:, i * P : (i + 1) * P], ident_bf[:])
+            nc.scalar.copy(out=prob_t[:, first * P : (first + WEIGHT_RUN) * P], in_=bank[:])
 
         wo_grouped = []
         wo_codes = []
@@ -134,7 +123,7 @@ def tile_model_pa_t_kernel(tc, attn_ctx, Wo, bo, cluster_probs, out):
                 out=wo_grouped[c][:, h * N_MOVE * PACK : (h + 1) * N_MOVE * PACK].rearrange(
                     "p (n i t) -> p n t i", i=4, t=PACK
                 ),
-                in_=wo_raw[c][:].rearrange("p (t h n i) -> p h n t i", t=PACK, h=HALVES, i=4)[:, h],
+                in_=wo_raw[(c, h)][:].rearrange("p (t n i) -> p n t i", t=PACK, i=4),
             )
 
         def quantise_wo(c, h):
@@ -152,22 +141,30 @@ def tile_model_pa_t_kernel(tc, attn_ctx, Wo, bo, cluster_probs, out):
         part_tiles = {}
 
         def weight(i, c):
-            return prob[:, TILES * c + i : TILES * c + i + 1]
+            return prob[:, C * i + c : C * i + c + 1]
 
         def bias_half(i, h):
             cols = slice(h * N_MOVE, (h + 1) * N_MOVE)
             bank = banks.tile([P, N_MOVE], F32)
             nc.tensor.matmul(
-                bank[:], lhsT=prob_sel[:, i * P : (i + 1) * P], rhs=bias_rows[:, cols], start=True, stop=True
+                bank[:], lhsT=prob_t[:, i * P : (i + 1) * P], rhs=bo_pad[:, cols], start=True, stop=True
             )
             nc.scalar.copy(out=res_tiles[i][:, cols], in_=bank[:])
 
         def scale_bias(i):
-            part_tiles[i] = work.tile([P, E], F32, name="part")
-            for c, row in ((0, res_tiles[i]), (1, part_tiles[i])):
-                nc.scalar.activation(
-                    out=row[:], in_=bias_all[:, c * E : (c + 1) * E], func=COPY, scale=weight(i, c)
-                )
+            nc.scalar.activation(out=res_tiles[i][:], in_=bias_all[:, 0:E], func=COPY, scale=weight(i, 0))
+
+        def scale_second_bias(i, h):
+            if h == 0:
+                part_tiles[i] = part_pool.tile([P, E], F32, name="part")
+            nc.gpsimd.tensor_scalar(
+                out=part_tiles[i][:, h * N_MOVE : (h + 1) * N_MOVE],
+                in0=bias_all[:, E + h * N_MOVE : E + (h + 1) * N_MOVE],
+                scalar1=weight(i, 1),
+                scalar2=0.0,
+                op0=MULT,
+                op1=ADD,
+            )
 
         def transpose_tokens(i):
             x, n, size = x_tiles[i]
@@ -178,26 +175,28 @@ def tile_model_pa_t_kernel(tc, attn_ctx, Wo, bo, cluster_probs, out):
                     s = 2 * j + u
                     first = (j * size + n) * WORDS + u * P
                     nc.tensor.transpose(bank[:, s * P : (s + 1) * P], x_words[:, first : first + P], ident[:])
-            grouped = work.tile([P, C * P * PACK], BF16, align_bytes=64)
+            if i % 2 == 0:
+                grouped_tiles[i // 2] = work.tile([P, 2 * C * P * PACK], BF16, name="grouped", align_bytes=64)
+            half = grouped_tiles[i // 2][:, (i % 2) * C * P * PACK : (i % 2 + 1) * C * P * PACK]
             nc.scalar.copy(
-                out=grouped[:].bitcast(F32).rearrange("p (c b s) -> p c b s", c=C, s=PACK),
+                out=half.bitcast(F32).rearrange("p (c b s) -> p c b s", c=C, s=PACK),
                 in_=bank[:].rearrange("p (s b c) -> p c b s", s=PACK, c=C),
             )
-            grouped_tiles[i] = grouped
 
-        def quantise_tokens(i):
-            codes = work.tile([P, C * P], U32, align_bytes=64)
-            scales = work.tile([P, C * P], U8, align_bytes=64)
-            nc.vector.quantize_mx(out=codes[:].bitcast(FP8X4), scales=scales[:], in_=grouped_tiles[i][:])
-            code_tiles[i] = (codes, scales)
+        def quantise_pair(j):
+            codes = work.tile([P, 2 * C * P], U32, align_bytes=64)
+            scales = work.tile([P, 2 * C * P], U8, align_bytes=64)
+            nc.vector.quantize_mx(out=codes[:].bitcast(FP8X4), scales=scales[:], in_=grouped_tiles[j][:])
+            code_tiles[j] = (codes, scales)
 
         def multiply(i, c, h):
-            codes, scales = code_tiles[i]
+            codes, scales = code_tiles[i // 2]
+            tokens = slice((C * (i % 2) + c) * P, (C * (i % 2) + c + 1) * P)
             bank = banks.tile([P, N_MOVE], F32)
             nc.tensor.matmul_mx(
                 out=bank[:],
-                lhsT=codes[:, c * P : (c + 1) * P].bitcast(FP8X4),
-                lhsT_scale=scales[:, c * P : (c + 1) * P],
+                lhsT=codes[:, tokens].bitcast(FP8X4),
+                lhsT_scale=scales[:, tokens],
                 rhs=wo_codes[c][:, h * N_MOVE : (h + 1) * N_MOVE].bitcast(FP8X4),
                 rhs_scale=wo_scales[c][:, h * N_MOVE : (h + 1) * N_MOVE],
                 start=True,
@@ -205,10 +204,14 @@ def tile_model_pa_t_kernel(tc, attn_ctx, Wo, bo, cluster_probs, out):
             )
             acc_tiles[(i, c, h)] = bank
 
-        def weigh_part(i):
-            part_tiles[i] = work.tile([P, E], F32, name="part")
+        def weigh_part(i, h):
+            if i not in part_tiles:
+                part_tiles[i] = part_pool.tile([P, E], F32, name="part")
             nc.scalar.activation(
-                out=part_tiles[i][:, 0:N_MOVE], in_=acc_tiles[(i, 0, 0)][:], func=COPY, scale=weight(i, 0)
+                out=part_tiles[i][:, h * N_MOVE : (h + 1) * N_MOVE],
+                in_=acc_tiles[(i, 0, h)][:],
+                func=COPY,
+                scale=weight(i, 0),
             )
 
         def combine(i, c, h):
@@ -218,16 +221,17 @@ def tile_model_pa_t_kernel(tc, attn_ctx, Wo, bo, cluster_probs, out):
             )
 
         def finish(i):
-            width = {"split": E, "shared": N_MOVE, "plain": 0}[kind(i)]
+            width = {"split": E, "double": E, "shared": N_MOVE, "plain": 0}[kind(i)]
             if width:
                 nc.gpsimd.tensor_tensor(
                     out=res_tiles[i][:, 0:width], in0=part_tiles[i][:, 0:width], in1=res_tiles[i][:, 0:width], op=ADD
                 )
             nc.sync.dma_start(out=out_rows[:, i, :], in_=res_tiles[i][:])
 
-        tensor_tiles = [i for i in range(TILES) if by_tensor(i)]
-        for i in tensor_tiles[:8]:
-            select_rows(i)
+        transpose_weights(0)
+        transpose_weights(8)
+        transpose_weights(16)
+        transpose_weights(24)
         group_wo(nc.vector.tensor_copy, 0, 0)
         group_wo(nc.vector.tensor_copy, 0, 1)
         quantise_wo(0, 0)
@@ -235,42 +239,64 @@ def tile_model_pa_t_kernel(tc, attn_ctx, Wo, bo, cluster_probs, out):
         transpose_tokens(0)
         transpose_tokens(1)
         group_wo(nc.vector.tensor_copy, 1, 0)
-        quantise_tokens(0)
+        quantise_pair(0)
         quantise_wo(1, 0)
         group_wo(nc.vector.tensor_copy, 1, 1)
-        for i in tensor_tiles[8:]:
-            select_rows(i)
         quantise_wo(1, 1)
 
         def make_res(i):
-            res_tiles[i] = res_pool.tile([P, E], F32, name="res")
+            if i not in res_tiles:
+                res_tiles[i] = res_pool.tile([P, E], F32, name="res")
 
-        for step in range(-1, TILES + 1):
-            bias, turned, quant, prod, done = step + 1, step + 3, step + 2, step, step - 1
-            if 2 <= turned < TILES:
+        def turned_by(step):
+            return min(TILES, step + 5 - step % 2 + 1)
+
+        def pairs_by(step):
+            return turned_by(step - 1) // 2
+
+        def product(reader, i, c, h):
+            multiply(i, c, h)
+            if reader == "S":
+                weigh_part(i, h)
+            else:
+                combine(i, c, h)
+
+        turned = 2
+        pairs = 1
+        for step in range(-2, TILES + 1):
+            bias, prod, done = step + 1, step, step - 1
+            while turned < turned_by(step):
                 transpose_tokens(turned)
+                turned += 1
+            for_scalar = []
+            for_vector = []
             if 0 <= bias < TILES:
                 make_res(bias)
-                if by_tensor(bias):
-                    bias_half(bias, 1)
+                if kind(bias) != "split":
+                    for_scalar.append((bias_half, bias, 1))
                 else:
                     scale_bias(bias)
             if 0 <= prod < TILES:
-                multiply(prod, 0, 1)
-                combine(prod, 0, 1)
-                multiply(prod, 0, 0)
-                if kind(prod) == "shared":
-                    weigh_part(prod)
-                else:
-                    combine(prod, 0, 0)
-            if 0 <= bias < TILES and by_tensor(bias):
-                bias_half(bias, 0)
-            if 0 <= prod < TILES:
-                multiply(prod, 1, 1)
-                combine(prod, 1, 1)
-                multiply(prod, 1, 0)
-                combine(prod, 1, 0)
-            if 1 <= quant < TILES:
-                quantise_tokens(quant)
+                for h in (1, 0):
+                    by_scalar = kind(prod) == "double" or kind(prod) == "shared" and h == 0
+                    if by_scalar:
+                        for_scalar.append((product, "S", prod, 0, h))
+                    else:
+                        for_vector.append((product, "V", prod, 0, h))
+                for_vector.append((product, "V", prod, 1, 1))
+                for_vector.append((product, "V", prod, 1, 0))
+            if 0 <= bias < TILES and kind(bias) != "split":
+                for_scalar.append((bias_half, bias, 0))
+            while for_scalar or for_vector:
+                for queue in (for_vector, for_scalar):
+                    if queue:
+                        call = queue.pop(0)
+                        call[0](*call[1:])
+            while pairs < pairs_by(step):
+                quantise_pair(pairs)
+                pairs += 1
             if 0 <= done:
                 finish(done)
+            for h, lead in ((0, 2), (1, 1)):
+                if 0 <= done + lead < TILES and kind(done + lead) == "split":
+                    scale_second_bias(done + lead, h)

@@ -30,7 +30,10 @@ FLOPS = 2 * B * C * L * K * E
 
 
 def kind(i):
-    return "plain" if i == TILES - 1 else "split" if i % 4 == 1 else "shared"
+    if i == TILES - 1:
+        return "plain"
+    return "split" if i % 4 == 3 else "shared"
+
 
 def tile_model_pa_t_kernel(tc, attn_ctx, Wo, bo, cluster_probs, out):
     nc = tc.nc
@@ -86,9 +89,10 @@ def tile_model_pa_t_kernel(tc, attn_ctx, Wo, bo, cluster_probs, out):
         load_wo(1, 0)
         load_wo(1, 1)
         load_x(1)
+        load_x(2)
         bias_all = const.tile([P, C * E], BF16)
         nc.sync.dma_start(out=bias_all[:], in_=bo.rearrange("c e -> (c e)").partition_broadcast(P))
-        for g in range(2, len(CHUNKS)):
+        for g in range(3, len(CHUNKS)):
             load_x(g)
 
         ident = const.tile([P, P], F32)
@@ -118,8 +122,8 @@ def tile_model_pa_t_kernel(tc, attn_ctx, Wo, bo, cluster_probs, out):
             wo_codes.append(const.tile([P, E], U32, name="wo_codes%d" % c, align_bytes=64))
             wo_scales.append(const.tile([P, E], U8, name="wo_scales%d" % c, align_bytes=64))
 
-        def group_wo(copy, c, h):
-            copy(
+        def group_wo(c, h):
+            nc.vector.tensor_copy(
                 out=wo_grouped[c][:, h * N_MOVE * PACK : (h + 1) * N_MOVE * PACK].rearrange(
                     "p (n i t) -> p n t i", i=4, t=PACK
                 ),
@@ -154,12 +158,11 @@ def tile_model_pa_t_kernel(tc, attn_ctx, Wo, bo, cluster_probs, out):
         def scale_bias(i):
             nc.scalar.activation(out=res_tiles[i][:], in_=bias_all[:, 0:E], func=COPY, scale=weight(i, 0))
 
-        def scale_second_bias(i, h):
-            if h == 0:
-                part_tiles[i] = part_pool.tile([P, E], F32, name="part")
+        def scale_second_bias(i):
+            part_tiles[i] = part_pool.tile([P, E], F32, name="part")
             nc.gpsimd.tensor_scalar(
-                out=part_tiles[i][:, h * N_MOVE : (h + 1) * N_MOVE],
-                in0=bias_all[:, E + h * N_MOVE : E + (h + 1) * N_MOVE],
+                out=part_tiles[i][:],
+                in0=bias_all[:, E : 2 * E],
                 scalar1=weight(i, 1),
                 scalar2=0.0,
                 op0=MULT,
@@ -205,8 +208,7 @@ def tile_model_pa_t_kernel(tc, attn_ctx, Wo, bo, cluster_probs, out):
             acc_tiles[(i, c, h)] = bank
 
         def weigh_part(i, h):
-            if i not in part_tiles:
-                part_tiles[i] = part_pool.tile([P, E], F32, name="part")
+            part_tiles[i] = part_pool.tile([P, E], F32, name="part")
             nc.scalar.activation(
                 out=part_tiles[i][:, h * N_MOVE : (h + 1) * N_MOVE],
                 in_=acc_tiles[(i, 0, h)][:],
@@ -215,88 +217,75 @@ def tile_model_pa_t_kernel(tc, attn_ctx, Wo, bo, cluster_probs, out):
             )
 
         def combine(i, c, h):
-            half = res_tiles[i][:, h * N_MOVE : (h + 1) * N_MOVE]
+            cols = slice(h * N_MOVE, (h + 1) * N_MOVE)
+            half = res_tiles[i][:, cols]
             nc.vector.scalar_tensor_tensor(
                 out=half, in0=acc_tiles[(i, c, h)][:], scalar=weight(i, c), in1=half, op0=MULT, op1=ADD
             )
+            if kind(i) == "plain" and c == 1:
+                nc.sync.dma_start(out=out_rows[:, i, cols], in_=half)
 
         def finish(i):
-            width = {"split": E, "double": E, "shared": N_MOVE, "plain": 0}[kind(i)]
-            if width:
-                nc.gpsimd.tensor_tensor(
-                    out=res_tiles[i][:, 0:width], in0=part_tiles[i][:, 0:width], in1=res_tiles[i][:, 0:width], op=ADD
-                )
+            width = E if kind(i) == "split" else N_MOVE
+            nc.gpsimd.tensor_tensor(
+                out=res_tiles[i][:, 0:width], in0=part_tiles[i][:, 0:width], in1=res_tiles[i][:, 0:width], op=ADD
+            )
             nc.sync.dma_start(out=out_rows[:, i, :], in_=res_tiles[i][:])
 
         transpose_weights(0)
-        transpose_weights(8)
-        transpose_weights(16)
-        transpose_weights(24)
-        group_wo(nc.vector.tensor_copy, 0, 0)
-        group_wo(nc.vector.tensor_copy, 0, 1)
+        group_wo(0, 0)
+        group_wo(0, 1)
         quantise_wo(0, 0)
         quantise_wo(0, 1)
         transpose_tokens(0)
         transpose_tokens(1)
-        group_wo(nc.vector.tensor_copy, 1, 0)
+        transpose_weights(8)
+        group_wo(1, 0)
         quantise_pair(0)
         quantise_wo(1, 0)
-        group_wo(nc.vector.tensor_copy, 1, 1)
+        group_wo(1, 1)
         quantise_wo(1, 1)
+        transpose_weights(16)
+        transpose_weights(24)
 
-        def make_res(i):
-            if i not in res_tiles:
-                res_tiles[i] = res_pool.tile([P, E], F32, name="res")
-
-        def turned_by(step):
-            return min(TILES, step + 5 - step % 2 + 1)
-
-        def pairs_by(step):
-            return turned_by(step - 1) // 2
-
-        def product(reader, i, c, h):
+        def read_by_scalar(i, c, h):
             multiply(i, c, h)
-            if reader == "S":
-                weigh_part(i, h)
-            else:
-                combine(i, c, h)
+            weigh_part(i, h)
 
-        turned = 2
-        pairs = 1
-        for step in range(-2, TILES + 1):
-            bias, prod, done = step + 1, step, step - 1
-            while turned < turned_by(step):
-                transpose_tokens(turned)
-                turned += 1
-            for_scalar = []
+        def read_by_vector(i, c, h):
+            multiply(i, c, h)
+            combine(i, c, h)
+
+        for step in range(-2, TILES):
+            if 0 <= step - 1 < TILES - 1:
+                finish(step - 1)
+            if 0 <= step + 1 < TILES and kind(step + 1) == "split":
+                scale_second_bias(step + 1)
             for_vector = []
-            if 0 <= bias < TILES:
-                make_res(bias)
-                if kind(bias) != "split":
-                    for_scalar.append((bias_half, bias, 1))
+            for_scalar = []
+            if 0 <= step + 1 < TILES:
+                res_tiles[step + 1] = res_pool.tile([P, E], F32, name="res")
+                if kind(step + 1) == "split":
+                    scale_bias(step + 1)
                 else:
-                    scale_bias(bias)
-            if 0 <= prod < TILES:
-                for h in (1, 0):
-                    by_scalar = kind(prod) == "double" or kind(prod) == "shared" and h == 0
-                    if by_scalar:
-                        for_scalar.append((product, "S", prod, 0, h))
-                    else:
-                        for_vector.append((product, "V", prod, 0, h))
-                for_vector.append((product, "V", prod, 1, 1))
-                for_vector.append((product, "V", prod, 1, 0))
-            if 0 <= bias < TILES and kind(bias) != "split":
-                for_scalar.append((bias_half, bias, 0))
-            while for_scalar or for_vector:
-                for queue in (for_vector, for_scalar):
-                    if queue:
-                        call = queue.pop(0)
-                        call[0](*call[1:])
-            while pairs < pairs_by(step):
-                quantise_pair(pairs)
-                pairs += 1
-            if 0 <= done:
-                finish(done)
-            for h, lead in ((0, 2), (1, 1)):
-                if 0 <= done + lead < TILES and kind(done + lead) == "split":
-                    scale_second_bias(done + lead, h)
+                    for_scalar.append((bias_half, step + 1, 1))
+            if 0 <= step < TILES:
+                for_vector.append((read_by_vector, step, 0, 1))
+                if kind(step) == "shared":
+                    for_scalar.append((read_by_scalar, step, 0, 0))
+                else:
+                    for_vector.append((read_by_vector, step, 0, 0))
+                for_vector.append((read_by_vector, step, 1, 1))
+                for_vector.append((read_by_vector, step, 1, 0))
+            if 0 <= step + 1 < TILES and kind(step + 1) != "split":
+                for_scalar.append((bias_half, step + 1, 0))
+            while for_vector or for_scalar:
+                for fills in (for_vector, for_scalar):
+                    if fills:
+                        fill = fills.pop(0)
+                        fill[0](*fill[1:])
+            if step % 2 == 0 and 2 <= step + 4 < TILES:
+                transpose_tokens(step + 4)
+                transpose_tokens(step + 5)
+            if step % 2 == 1 and 2 <= step + 3 < TILES:
+                quantise_pair((step + 3) // 2)

@@ -32,7 +32,7 @@ FLOPS = 2 * B * C * L * K * E
 def kind(i):
     if i == TILES - 1:
         return "plain"
-    return "split" if i % 4 == 3 else "shared"
+    return "split" if i % 4 == 2 and i < 28 else "shared"
 
 
 def tile_model_pa_t_kernel(tc, attn_ctx, Wo, bo, cluster_probs, out):
@@ -47,7 +47,7 @@ def tile_model_pa_t_kernel(tc, attn_ctx, Wo, bo, cluster_probs, out):
         const = ctx.enter_context(tc.tile_pool(name="const", bufs=1))
         work = ctx.enter_context(tc.tile_pool(name="work", bufs=4))
         part_pool = ctx.enter_context(tc.tile_pool(name="part_pool", bufs=5))
-        res_pool = ctx.enter_context(tc.tile_pool(name="res_pool", bufs=9))
+        res_pool = ctx.enter_context(tc.tile_pool(name="res_pool", bufs=11))
         banks = ctx.enter_context(tc.psum_pool(name="banks", bufs=8))
         ctx.enter_context(tc.manual_schedule())
 
@@ -256,29 +256,31 @@ def tile_model_pa_t_kernel(tc, attn_ctx, Wo, bo, cluster_probs, out):
             multiply(i, c, h)
             combine(i, c, h)
 
-        for step in range(-2, TILES):
-            if 0 <= step - 1 < TILES - 1:
-                finish(step - 1)
-            if 0 <= step + 1 < TILES and kind(step + 1) == "split":
-                scale_second_bias(step + 1)
+        for step in range(-2, TILES + 1):
+            bias, first, second = step + 2, step, step - 1
+            if 0 <= second - 1:
+                finish(second - 1)
+            if 0 <= second + 1 < TILES and kind(second + 1) == "split":
+                scale_second_bias(second + 1)
             for_vector = []
             for_scalar = []
-            if 0 <= step + 1 < TILES:
-                res_tiles[step + 1] = res_pool.tile([P, E], F32, name="res")
-                if kind(step + 1) == "split":
-                    scale_bias(step + 1)
+            if 0 <= bias < TILES:
+                res_tiles[bias] = res_pool.tile([P, E], F32, name="res")
+                if kind(bias) == "split":
+                    scale_bias(bias)
                 else:
-                    for_scalar.append((bias_half, step + 1, 1))
-            if 0 <= step < TILES:
-                for_vector.append((read_by_vector, step, 0, 1))
-                if kind(step) == "shared":
-                    for_scalar.append((read_by_scalar, step, 0, 0))
+                    for_scalar.append((bias_half, bias, 1))
+            if 0 <= first < TILES:
+                for_vector.append((read_by_vector, first, 0, 1))
+                if kind(first) == "shared":
+                    for_scalar.append((read_by_scalar, first, 0, 0))
                 else:
-                    for_vector.append((read_by_vector, step, 0, 0))
-                for_vector.append((read_by_vector, step, 1, 1))
-                for_vector.append((read_by_vector, step, 1, 0))
-            if 0 <= step + 1 < TILES and kind(step + 1) != "split":
-                for_scalar.append((bias_half, step + 1, 0))
+                    for_vector.append((read_by_vector, first, 0, 0))
+            if 0 <= second < TILES:
+                for_vector.append((read_by_vector, second, 1, 1))
+                for_vector.append((read_by_vector, second, 1, 0))
+            if 0 <= bias < TILES and kind(bias) != "split":
+                for_scalar.append((bias_half, bias, 0))
             while for_vector or for_scalar:
                 for fills in (for_vector, for_scalar):
                     if fills:

@@ -30,7 +30,7 @@ FLOPS = 2 * B * C * L * K * E
 
 
 def kind(i):
-    if i == TILES - 1:
+    if i >= TILES - 2:
         return "plain"
     return "split" if i % 4 == 2 and i < 28 else "shared"
 
@@ -222,31 +222,32 @@ def tile_model_pa_t_kernel(tc, attn_ctx, Wo, bo, cluster_probs, out):
             nc.vector.scalar_tensor_tensor(
                 out=half, in0=acc_tiles[(i, c, h)][:], scalar=weight(i, c), in1=half, op0=MULT, op1=ADD
             )
-            if kind(i) == "plain" and c == 1:
+            if i == TILES - 1 and c == 1:
                 nc.sync.dma_start(out=out_rows[:, i, cols], in_=half)
 
         def finish(i):
-            width = E if kind(i) == "split" else N_MOVE
-            nc.gpsimd.tensor_tensor(
-                out=res_tiles[i][:, 0:width], in0=part_tiles[i][:, 0:width], in1=res_tiles[i][:, 0:width], op=ADD
-            )
+            if kind(i) != "plain":
+                width = E if kind(i) == "split" else N_MOVE
+                nc.gpsimd.tensor_tensor(
+                    out=res_tiles[i][:, 0:width], in0=part_tiles[i][:, 0:width], in1=res_tiles[i][:, 0:width], op=ADD
+                )
             nc.sync.dma_start(out=out_rows[:, i, :], in_=res_tiles[i][:])
 
         transpose_weights(0)
+        transpose_weights(8)
         group_wo(0, 0)
         group_wo(0, 1)
         quantise_wo(0, 0)
         quantise_wo(0, 1)
         transpose_tokens(0)
         transpose_tokens(1)
-        transpose_weights(8)
-        group_wo(1, 0)
-        quantise_pair(0)
-        quantise_wo(1, 0)
-        group_wo(1, 1)
-        quantise_wo(1, 1)
         transpose_weights(16)
         transpose_weights(24)
+        group_wo(1, 0)
+        quantise_wo(1, 0)
+        group_wo(1, 1)
+        quantise_pair(0)
+        quantise_wo(1, 1)
 
         def read_by_scalar(i, c, h):
             multiply(i, c, h)

@@ -63,15 +63,13 @@ def tile_model_pa_t_kernel(tc, attn_ctx, Wo, bo, cluster_probs, out):
         wo_raw = {}
         x_tiles = {}
 
-        def load_wo(c, h):
-            raw = const.tile([P, PACK * N_MOVE], BF16, name="wo_raw%d%d" % (c, h))
-            for u in range(2):
-                rows = wo_rows[c][2 * P * u : 2 * P * (u + 1), h * N_MOVE : (h + 1) * N_MOVE]
-                nc.sync.dma_start(
-                    out=raw[:, 2 * N_MOVE * u : 2 * N_MOVE * (u + 1)].rearrange("p (r e) -> p r e", r=2),
-                    in_=rows.rearrange("(p r) e -> p r e", r=2),
-                )
-            wo_raw[(c, h)] = raw
+        def load_wo(c):
+            raw = const.tile([P, PACK * E], BF16, name="wo_raw%d" % c)
+            nc.sync.dma_start(
+                out=raw[:].rearrange("p (u f) -> p u f", u=2),
+                in_=wo_rows[c].rearrange("(u p r) e -> p u (r e)", u=2, r=2),
+            )
+            wo_raw[c] = raw
 
         def load_x(g):
             first, size = sum(CHUNKS[:g]), CHUNKS[g]
@@ -83,11 +81,9 @@ def tile_model_pa_t_kernel(tc, attn_ctx, Wo, bo, cluster_probs, out):
             for n in range(size):
                 x_tiles[first + n] = (x, n, size)
 
-        load_wo(0, 0)
-        load_wo(0, 1)
+        load_wo(0)
         load_x(0)
-        load_wo(1, 0)
-        load_wo(1, 1)
+        load_wo(1)
         load_x(1)
         load_x(2)
         bias_all = const.tile([P, C * E], BF16)
@@ -127,7 +123,7 @@ def tile_model_pa_t_kernel(tc, attn_ctx, Wo, bo, cluster_probs, out):
                 out=wo_grouped[c][:, h * N_MOVE * PACK : (h + 1) * N_MOVE * PACK].rearrange(
                     "p (n i t) -> p n t i", i=4, t=PACK
                 ),
-                in_=wo_raw[(c, h)][:].rearrange("p (t n i) -> p n t i", t=PACK, i=4),
+                in_=wo_raw[c][:].rearrange("p (t h n i) -> p h n t i", t=PACK, h=HALVES, i=4)[:, h],
             )
 
         def quantise_wo(c, h):

from contextlib import ExitStack

import concourse.mybir as mybir
from concourse.masks import make_identity

F32 = mybir.dt.float32
BF16 = mybir.dt.bfloat16
U32 = mybir.dt.uint32
U8 = mybir.dt.uint8
FP8X4 = mybir.dt.float8_e4m3fn_x4
MULT = mybir.AluOpType.mult
ADD = mybir.AluOpType.add
COPY = mybir.ActivationFunctionType.Copy

B = 64
C = 2
L = 64
K = 512
E = 1024
P = 128
PACK = 4
WORDS = K // 2
N_MOVE = 512
HALVES = E // N_MOVE
TILES = B * L // P
BO_ROW = 32
WEIGHT_RUN = 8
CHUNKS = (2, 2, 4, 4, 4, 4, 4, 4, 4)
FLOPS = 2 * B * C * L * K * E


def kind(i):
    if i >= TILES - 2:
        return "plain"
    return "split" if i % 4 == 2 and i < 28 else "shared"


def tile_model_pa_t_kernel(tc, attn_ctx, Wo, bo, cluster_probs, out):
    nc = tc.nc

    out_rows = out.rearrange("b (j i) e -> (b j) i e", j=2)
    prob_rows = cluster_probs.rearrange("b (j i) c -> (b j) (i c)", j=2)
    attn_rows = attn_ctx.rearrange("b c (j i) h d -> (b c) j (i h d)", j=2)
    wo_rows = Wo.rearrange("c h d e -> c (h d) e")

    with ExitStack() as ctx:
        const = ctx.enter_context(tc.tile_pool(name="const", bufs=1))
        work = ctx.enter_context(tc.tile_pool(name="work", bufs=4))
        part_pool = ctx.enter_context(tc.tile_pool(name="part_pool", bufs=5))
        res_pool = ctx.enter_context(tc.tile_pool(name="res_pool", bufs=11))
        banks = ctx.enter_context(tc.psum_pool(name="banks", bufs=8))
        ctx.enter_context(tc.manual_schedule())

        prob_bf = const.tile([P, TILES * C], BF16)
        nc.scalar.dma_start(out=prob_bf[:], in_=prob_rows)
        bo_pad = const.tile([P, E], BF16)
        nc.vector.memset(bo_pad[:].bitcast(U32), 0)
        for c in range(C):
            nc.scalar.dma_start(out=bo_pad[c * BO_ROW : c * BO_ROW + 1, :], in_=bo[c : c + 1, :])
        prob_wide = const.tile([P, TILES * P], BF16)
        nc.vector.memset(prob_wide[:].bitcast(U32), 0)

        wo_raw = {}
        x_tiles = {}

        def load_wo(c):
            raw = const.tile([P, PACK * E], BF16, name="wo_raw%d" % c)
            nc.sync.dma_start(
                out=raw[:].rearrange("p (u f) -> p u f", u=2),
                in_=wo_rows[c].rearrange("(u p r) e -> p u (r e)", u=2, r=2),
            )
            wo_raw[c] = raw

        def load_x(g):
            first, size = sum(CHUNKS[:g]), CHUNKS[g]
            x = const.tile([P, 2 * size * K], BF16, name="x%d" % g)
            nc.sync.dma_start(
                out=x[:].rearrange("p (j f) -> p j f", j=2),
                in_=attn_rows[:, :, first * K : (first + size) * K],
            )
            for n in range(size):
                x_tiles[first + n] = (x, n, size)

        load_wo(0)
        load_x(0)
        load_wo(1)
        load_x(1)
        load_x(2)
        bias_all = const.tile([P, C * E], BF16)
        nc.sync.dma_start(out=bias_all[:], in_=bo.rearrange("c e -> (c e)").partition_broadcast(P))
        for g in range(3, len(CHUNKS)):
            load_x(g)

        ident = const.tile([P, P], F32)
        make_identity(nc, ident[:])
        ident_bf = const.tile([P, P], BF16)
        nc.vector.tensor_copy(out=ident_bf[:], in_=ident[:])
        prob = const.tile([P, TILES * C], F32)
        nc.vector.tensor_copy(out=prob[:], in_=prob_bf[:])
        nc.vector.tensor_copy(
            out=prob_wide[:].rearrange("p (i w) -> p i w", w=P)[:, :, 0 : C * BO_ROW : BO_ROW],
            in_=prob_bf[:].rearrange("p (i c) -> p i c", c=C),
        )
        prob_t = const.tile([P, TILES * P], BF16)

        def transpose_weights(first):
            bank = banks.tile([P, WEIGHT_RUN * P], BF16)
            for n in range(WEIGHT_RUN):
                i = first + n
                nc.tensor.transpose(bank[:, n * P : (n + 1) * P], prob_wide[:, i * P : (i + 1) * P], ident_bf[:])
            nc.scalar.copy(out=prob_t[:, first * P : (first + WEIGHT_RUN) * P], in_=bank[:])

        wo_grouped = []
        wo_codes = []
        wo_scales = []
        for c in range(C):
            wo_grouped.append(const.tile([P, E * PACK], BF16, name="wo_grouped%d" % c, align_bytes=64))
            wo_codes.append(const.tile([P, E], U32, name="wo_codes%d" % c, align_bytes=64))
            wo_scales.append(const.tile([P, E], U8, name="wo_scales%d" % c, align_bytes=64))

        def group_wo(c, h):
            nc.vector.tensor_copy(
                out=wo_grouped[c][:, h * N_MOVE * PACK : (h + 1) * N_MOVE * PACK].rearrange(
                    "p (n i t) -> p n t i", i=4, t=PACK
                ),
                in_=wo_raw[c][:].rearrange("p (t h n i) -> p h n t i", t=PACK, h=HALVES, i=4)[:, h],
            )

        def quantise_wo(c, h):
            cols = slice(h * N_MOVE, (h + 1) * N_MOVE)
            nc.vector.quantize_mx(
                out=wo_codes[c][:, cols].bitcast(FP8X4),
                scales=wo_scales[c][:, cols],
                in_=wo_grouped[c][:, h * N_MOVE * PACK : (h + 1) * N_MOVE * PACK],
            )

        res_tiles = {}
        grouped_tiles = {}
        code_tiles = {}
        acc_tiles = {}
        part_tiles = {}

        def weight(i, c):
            return prob[:, C * i + c : C * i + c + 1]

        def bias_half(i, h):
            cols = slice(h * N_MOVE, (h + 1) * N_MOVE)
            bank = banks.tile([P, N_MOVE], F32)
            nc.tensor.matmul(
                bank[:], lhsT=prob_t[:, i * P : (i + 1) * P], rhs=bo_pad[:, cols], start=True, stop=True
            )
            nc.scalar.copy(out=res_tiles[i][:, cols], in_=bank[:])

        def scale_bias(i):
            nc.scalar.activation(out=res_tiles[i][:], in_=bias_all[:, 0:E], func=COPY, scale=weight(i, 0))

        def scale_second_bias(i):
            part_tiles[i] = part_pool.tile([P, E], F32, name="part")
            nc.gpsimd.tensor_scalar(
                out=part_tiles[i][:],
                in0=bias_all[:, E : 2 * E],
                scalar1=weight(i, 1),
                scalar2=0.0,
                op0=MULT,
                op1=ADD,
            )

        def transpose_tokens(i):
            x, n, size = x_tiles[i]
            x_words = x[:].bitcast(F32)
            bank = banks.tile([P, PACK * P], F32)
            for j in range(2):
                for u in range(2):
                    s = 2 * j + u
                    first = (j * size + n) * WORDS + u * P
                    nc.tensor.transpose(bank[:, s * P : (s + 1) * P], x_words[:, first : first + P], ident[:])
            if i % 2 == 0:
                grouped_tiles[i // 2] = work.tile([P, 2 * C * P * PACK], BF16, name="grouped", align_bytes=64)
            half = grouped_tiles[i // 2][:, (i % 2) * C * P * PACK : (i % 2 + 1) * C * P * PACK]
            nc.scalar.copy(
                out=half.bitcast(F32).rearrange("p (c b s) -> p c b s", c=C, s=PACK),
                in_=bank[:].rearrange("p (s b c) -> p c b s", s=PACK, c=C),
            )

        def quantise_pair(j):
            codes = work.tile([P, 2 * C * P], U32, align_bytes=64)
            scales = work.tile([P, 2 * C * P], U8, align_bytes=64)
            nc.vector.quantize_mx(out=codes[:].bitcast(FP8X4), scales=scales[:], in_=grouped_tiles[j][:])
            code_tiles[j] = (codes, scales)

        def multiply(i, c, h):
            codes, scales = code_tiles[i // 2]
            tokens = slice((C * (i % 2) + c) * P, (C * (i % 2) + c + 1) * P)
            bank = banks.tile([P, N_MOVE], F32)
            nc.tensor.matmul_mx(
                out=bank[:],
                lhsT=codes[:, tokens].bitcast(FP8X4),
                lhsT_scale=scales[:, tokens],
                rhs=wo_codes[c][:, h * N_MOVE : (h + 1) * N_MOVE].bitcast(FP8X4),
                rhs_scale=wo_scales[c][:, h * N_MOVE : (h + 1) * N_MOVE],
                start=True,
                stop=True,
            )
            acc_tiles[(i, c, h)] = bank

        def weigh_part(i, h):
            part_tiles[i] = part_pool.tile([P, E], F32, name="part")
            nc.scalar.activation(
                out=part_tiles[i][:, h * N_MOVE : (h + 1) * N_MOVE],
                in_=acc_tiles[(i, 0, h)][:],
                func=COPY,
                scale=weight(i, 0),
            )

        def combine(i, c, h):
            cols = slice(h * N_MOVE, (h + 1) * N_MOVE)
            half = res_tiles[i][:, cols]
            nc.vector.scalar_tensor_tensor(
                out=half, in0=acc_tiles[(i, c, h)][:], scalar=weight(i, c), in1=half, op0=MULT, op1=ADD
            )
            if i == TILES - 1 and c == 1:
                nc.sync.dma_start(out=out_rows[:, i, cols], in_=half)

        def finish(i):
            if kind(i) != "plain":
                width = E if kind(i) == "split" else N_MOVE
                nc.gpsimd.tensor_tensor(
                    out=res_tiles[i][:, 0:width], in0=part_tiles[i][:, 0:width], in1=res_tiles[i][:, 0:width], op=ADD
                )
            nc.sync.dma_start(out=out_rows[:, i, :], in_=res_tiles[i][:])

        transpose_weights(0)
        transpose_weights(8)
        group_wo(0, 0)
        group_wo(0, 1)
        quantise_wo(0, 0)
        quantise_wo(0, 1)
        transpose_tokens(0)
        transpose_tokens(1)
        transpose_weights(16)
        transpose_weights(24)
        group_wo(1, 0)
        quantise_wo(1, 0)
        group_wo(1, 1)
        quantise_pair(0)
        quantise_wo(1, 1)

        def read_by_scalar(i, c, h):
            multiply(i, c, h)
            weigh_part(i, h)

        def read_by_vector(i, c, h):
            multiply(i, c, h)
            combine(i, c, h)

        for step in range(-2, TILES + 1):
            bias, first, second = step + 2, step, step - 1
            if 0 <= second - 1:
                finish(second - 1)
            if 0 <= second + 1 < TILES and kind(second + 1) == "split":
                scale_second_bias(second + 1)
            for_vector = []
            for_scalar = []
            if 0 <= bias < TILES:
                res_tiles[bias] = res_pool.tile([P, E], F32, name="res")
                if kind(bias) == "split":
                    scale_bias(bias)
                else:
                    for_scalar.append((bias_half, bias, 1))
            if 0 <= first < TILES:
                for_vector.append((read_by_vector, first, 0, 1))
                if kind(first) == "shared":
                    for_scalar.append((read_by_scalar, first, 0, 0))
                else:
                    for_vector.append((read_by_vector, first, 0, 0))
            if 0 <= second < TILES:
                for_vector.append((read_by_vector, second, 1, 1))
                for_vector.append((read_by_vector, second, 1, 0))
            if 0 <= bias < TILES and kind(bias) != "split":
                for_scalar.append((bias_half, bias, 0))
            while for_vector or for_scalar:
                for fills in (for_vector, for_scalar):
                    if fills:
                        fill = fills.pop(0)
                        fill[0](*fill[1:])
            if step % 2 == 0 and 2 <= step + 4 < TILES:
                transpose_tokens(step + 4)
                transpose_tokens(step + 5)
            if step % 2 == 1 and 2 <= step + 3 < TILES:
                quantise_pair((step + 3) // 2)
